import numpy as np
import ml_dtypes


def mxq(x, axis, fmt="e4m3"):
    dtype, down = {"e4m3": (ml_dtypes.float8_e4m3fn, 7), "e5m2": (ml_dtypes.float8_e5m2, 14)}[fmt]
    v = np.moveaxis(np.asarray(x, np.float32).astype(ml_dtypes.bfloat16).astype(np.float64), axis, -1)
    blocks = v.reshape(v.shape[:-1] + (-1, 32))
    amax = np.abs(blocks).max(-1, keepdims=True)
    byte = np.maximum(np.where(amax > 0, np.frexp(amax)[1] - 1 + 127, 0) - down, 1)
    scale = np.exp2(byte - 127.0)
    codes = (blocks / scale).astype(np.float32).astype(dtype).astype(np.float64)
    return np.moveaxis((codes * scale).reshape(v.shape), -1, axis)


WIDE = False


def mx_kscale(k):
    if not WIDE:
        return np.ones(k)
    levels = np.array([10, -10, 5, -5, 0])
    a = np.random.permutation(np.resize(levels, k // 512 * 4)).reshape(k // 512, 4)
    idx = np.arange(k)
    return np.exp2(a[idx // 512, idx % 128 // 32])


BF16 = ml_dtypes.bfloat16


def bf(x):
    return np.asarray(x, np.float32).astype(BF16)


def f64(x):
    return np.asarray(x).astype(np.float64)


B, IN, OUT, NK, DEG = 2048, 1024, 128, 10, 3
K0 = NK + DEG
JIT = 0.25


def b_spline_basis(x, t, degree):
    n0 = t.shape[0] - 1
    xe = x[..., None]
    basis = ((xe >= t[:-1]) & (xe < t[1:])).astype(np.float64)
    for p in range(1, degree + 1):
        ti = t[: n0 - p]
        tip = t[p:n0]
        ti1 = t[1 : n0 - p + 1]
        tip1 = t[p + 1 : n0 + 1]
        d1 = np.where(tip - ti > 0, tip - ti, np.ones_like(ti))
        d2 = np.where(tip1 - ti1 > 0, tip1 - ti1, np.ones_like(ti1))
        left = np.where(tip - ti > 0, (xe - ti) / d1, 0.0) * basis[..., : n0 - p]
        right = np.where(tip1 - ti1 > 0, (tip1 - xe) / d2, 0.0) * basis[..., 1 : n0 - p + 1]
        new = left + right
        pad = np.zeros(x.shape + (p,))
        basis = np.concatenate([new, pad], axis=-1)
    return basis


def setup_inputs():
    knots = np.linspace(0.0, 1.0, K0 + 1)
    knots[1:-1] += np.random.uniform(-JIT, JIT, K0 - 1) / K0
    s = mx_kscale(NK * IN)[:IN]
    g0 = np.exp2(np.round(np.log2((1.0 - JIT) / K0) - 0.5))
    c0 = np.exp2(np.round(np.log2(np.prod(np.arange(1, DEG + 1) / K0)) + 0.5))
    g = np.where(s < 1.0, g0 * s, 1.0)
    h = np.where(s < 1.0, c0 / g**DEG, 1.0)
    x = np.random.uniform(0.0, 1.0, (B, IN)) * g[None, :]
    cp = np.random.standard_normal((OUT, IN, K0)) * 1.5 / np.sqrt(IN)
    cp[:, :, 0] *= h[None, :]
    return {"x": bf(x), "knots": bf(knots), "control_points": bf(cp)}


def reference(x, knots, control_points):
    basis = b_spline_basis(f64(x), f64(knots), DEG)
    a = basis[:, :, :NK].transpose(0, 2, 1).reshape(B, NK * IN)
    w = f64(control_points)[:, :, :NK].transpose(2, 1, 0).reshape(NK * IN, OUT)
    return mxq(a, 1, "e4m3") @ mxq(w, 0, "e4m3")

@@ -1,0 +1,226 @@
+from contextlib import ExitStack
+
+import concourse.mybir as mybir
+from concourse.masks import make_identity
+
+F32 = mybir.dt.float32
+BF16 = mybir.dt.bfloat16
+U32 = mybir.dt.uint32
+U8 = mybir.dt.uint8
+FP8X4 = mybir.dt.float8_e4m3fn_x4
+ALU = mybir.AluOpType
+ACT = mybir.ActivationFunctionType
+
+P = 128
+PACK = 4
+BATCH = 2048
+FEATURES = 1024
+OUTPUTS = 128
+KNOTS = 14
+POINTS = 13
+BASES = 10
+HALVES = FEATURES // (P * PACK)
+ROWS = 512
+ROW_TILES = ROWS // P
+ROUNDS = BATCH // ROWS
+CHUNK = ROWS * PACK
+
+FLOPS = 2 * BATCH * BASES * FEATURES * OUTPUTS
+
+
+def spline_constants(nc, pool, knots):
+    knots_bf = pool.tile([P, KNOTS], BF16)
+    nc.sync.dma_start(out=knots_bf[:], in_=knots.partition_broadcast(P))
+    t = pool.tile([P, KNOTS], F32)
+    nc.vector.tensor_copy(out=t[:], in_=knots_bf[:])
+    neg_t = pool.tile([P, KNOTS], F32)
+    nc.vector.tensor_scalar_mul(out=neg_t[:], in0=t[:], scalar1=-1.0)
+
+    d1 = pool.tile([P, KNOTS - 1], F32)
+    d2 = pool.tile([P, KNOTS - 2], F32)
+    d3 = pool.tile([P, KNOTS - 3], F32)
+    d4 = pool.tile([P, KNOTS - 4], F32)
+    for step, diff in ((1, d1), (2, d2), (3, d3), (4, d4)):
+        nc.vector.tensor_sub(out=diff[:], in0=t[:, step:KNOTS], in1=t[:, 0 : KNOTS - step])
+
+    cubes = KNOTS - 3
+    p_prod = pool.tile([P, cubes], F32)
+    nc.vector.tensor_mul(out=p_prod[:], in0=d1[:, 0:cubes], in1=d2[:, 0:cubes])
+    nc.vector.tensor_mul(out=p_prod[:], in0=p_prod[:], in1=d3[:, 0:cubes])
+    p_scale = pool.tile([P, cubes], F32)
+    nc.vector.reciprocal(out=p_scale[:], in_=p_prod[:])
+    q_prod = pool.tile([P, cubes], F32)
+    nc.vector.tensor_mul(out=q_prod[:], in0=d1[:, 2 : 2 + cubes], in1=d2[:, 1 : 1 + cubes])
+    nc.vector.tensor_mul(out=q_prod[:], in0=q_prod[:], in1=d3[:, 0:cubes])
+    q_recip = pool.tile([P, cubes], F32)
+    nc.vector.reciprocal(out=q_recip[:], in_=q_prod[:])
+    q_scale = pool.tile([P, cubes], F32)
+    nc.vector.tensor_scalar_mul(out=q_scale[:], in0=q_recip[:], scalar1=-1.0)
+
+    d1_recip = pool.tile([P, KNOTS - 1], F32)
+    nc.vector.reciprocal(out=d1_recip[:], in_=d1[:])
+    neg_d4 = pool.tile([P, BASES], F32)
+    nc.vector.tensor_scalar_mul(out=neg_d4[:], in0=d4[:], scalar1=-1.0)
+    left_w = pool.tile([P, BASES], F32)
+    nc.vector.tensor_mul(out=left_w[:], in0=neg_d4[:], in1=d1_recip[:, 0:BASES])
+    right_w = pool.tile([P, BASES], F32)
+    nc.vector.tensor_mul(out=right_w[:], in0=neg_d4[:], in1=d1_recip[:, 3 : 3 + BASES])
+    return {
+        "t": t,
+        "neg_t": neg_t,
+        "p_scale": p_scale,
+        "q_scale": q_scale,
+        "left_w": left_w,
+        "right_w": right_w,
+    }
+
+
+def tile_kanlayer_kernel(tc, x, knots, control_points, out):
+    nc = tc.nc
+    with ExitStack() as ctx:
+        consts = ctx.enter_context(tc.tile_pool(name="consts", bufs=1))
+        weights = ctx.enter_context(tc.tile_pool(name="weights", bufs=1))
+        stage = ctx.enter_context(tc.tile_pool(name="stage", bufs=2))
+        x_pool = ctx.enter_context(tc.tile_pool(name="x_pool", bufs=ROW_TILES))
+        cube_pool = ctx.enter_context(tc.tile_pool(name="cube_pool", bufs=3))
+        left_pool = ctx.enter_context(tc.tile_pool(name="left_pool", bufs=6))
+        mx_pool = ctx.enter_context(tc.tile_pool(name="mx_pool", bufs=3))
+        flip_psum = ctx.enter_context(tc.psum_pool(name="flip_psum", bufs=3))
+        acc_psum = ctx.enter_context(tc.psum_pool(name="acc_psum", bufs=1))
+
+        ident = consts.tile([P, P], BF16)
+        make_identity(nc, ident[:])
+        c = spline_constants(nc, consts, knots)
+
+        def load_rows(r):
+            tiles = []
+            for m in range(ROW_TILES):
+                x_sb = x_pool.tile([P, FEATURES], BF16, name="x_sb")
+                first = r * ROWS + m * P
+                nc.sync.dma_start(out=x_sb[:], in_=x[first : first + P, :])
+                tiles.append(x_sb)
+            return tiles
+
+        x_first = load_rows(0)
+
+        cp_sb = weights.tile([P, FEATURES, POINTS], BF16)
+        nc.sync.dma_start(out=cp_sb[:], in_=control_points)
+        w_codes = weights.tile([P, BASES, HALVES * OUTPUTS], U32, align_bytes=64)
+        w_scales = weights.tile([P, BASES, HALVES * OUTPUTS], U8, align_bytes=64)
+        for k in range(BASES):
+            w_flip = flip_psum.tile([P, HALVES * PACK, P], BF16, name="flip")
+            for n in range(HALVES * PACK):
+                nc.tensor.transpose(w_flip[:, n, :], cp_sb[:, n * P : (n + 1) * P, k], ident[:])
+            w_grouped = stage.tile([P, HALVES, OUTPUTS, PACK], BF16, align_bytes=64)
+            nc.scalar.copy(
+                out=w_grouped[:], in_=w_flip[:].rearrange("p (g t) o -> p g o t", g=HALVES)
+            )
+            nc.vector.quantize_mx(
+                out=w_codes[:, k, :].bitcast(FP8X4),
+                scales=w_scales[:, k, :],
+                in_=w_grouped[:].rearrange("p g o t -> p (g o t)"),
+            )
+
+        for r in range(ROUNDS):
+            x_tiles = x_first if r == 0 else load_rows(r)
+            v = stage.tile([P, HALVES, ROWS, PACK], BF16)
+            for m in range(ROW_TILES):
+                x_flip = flip_psum.tile([P, HALVES * PACK, P], BF16, name="flip")
+                for n in range(HALVES * PACK):
+                    nc.tensor.transpose(
+                        x_flip[:, n, :], x_tiles[m][:, n * P : (n + 1) * P], ident[:]
+                    )
+                nc.scalar.copy(
+                    out=v[:, :, m * P : (m + 1) * P, :],
+                    in_=x_flip[:].rearrange("p (g t) b -> p g b t", g=HALVES),
+                )
+
+            acc = [
+                acc_psum.tile([P, OUTPUTS], F32, name="acc%d" % m) for m in range(ROW_TILES)
+            ]
+            for g in range(HALVES):
+                vg = v[:, g, :, :].rearrange("p b t -> p (b t)")
+                p_cube = {}
+                q_cube = {}
+                left = {}
+                for i in range(KNOTS):
+                    square = cube_pool.tile([P, CHUNK], F32)
+                    nc.scalar.activation(
+                        out=square[:], in_=vg, func=ACT.Square, bias=c["neg_t"][:, i : i + 1]
+                    )
+                    cube = cube_pool.tile([P, CHUNK], F32)
+                    nc.vector.scalar_tensor_tensor(
+                        out=cube[:],
+                        in0=vg,
+                        scalar=c["t"][:, i : i + 1],
+                        in1=square[:],
+                        op0=ALU.subtract,
+                        op1=ALU.mult,
+                    )
+                    if i <= KNOTS - 4:
+                        p_cube[i] = cube_pool.tile([P, CHUNK], F32, name="p_cube")
+                        nc.scalar.activation(
+                            out=p_cube[i][:],
+                            in_=cube[:],
+                            func=ACT.Relu,
+                            scale=c["p_scale"][:, i : i + 1],
+                        )
+                    if i >= 3:
+                        q_cube[i] = cube_pool.tile([P, CHUNK], F32, name="q_cube")
+                        nc.scalar.activation(
+                            out=q_cube[i][:],
+                            in_=cube[:],
+                            func=ACT.Relu,
+                            scale=c["q_scale"][:, i - 3 : i - 2],
+                        )
+                    if 1 <= i <= BASES:
+                        k = i - 1
+                        left[k] = left_pool.tile([P, CHUNK], BF16, name="left")
+                        nc.vector.scalar_tensor_tensor(
+                            out=left[k][:],
+                            in0=p_cube[k + 1][:],
+                            scalar=c["left_w"][:, k : k + 1],
+                            in1=p_cube[k][:],
+                            op0=ALU.mult,
+                            op1=ALU.add,
+                        )
+                    if i >= 4:
+                        k = i - 4
+                        right = stage.tile([P, CHUNK], BF16)
+                        nc.vector.scalar_tensor_tensor(
+                            out=right[:],
+                            in0=q_cube[k + 3][:],
+                            scalar=c["right_w"][:, k : k + 1],
+                            in1=q_cube[k + 4][:],
+                            op0=ALU.mult,
+                            op1=ALU.add,
+                        )
+                        basis = mx_pool.tile([P, CHUNK], BF16, align_bytes=64)
+                        nc.vector.tensor_tensor(
+                            out=basis[:], in0=left[k][:], in1=right[:], op=ALU.max
+                        )
+                        b_codes = mx_pool.tile([P, ROWS], U32, align_bytes=64)
+                        b_scales = mx_pool.tile([P, ROWS], U8, align_bytes=64)
+                        nc.vector.quantize_mx(
+                            out=b_codes[:].bitcast(FP8X4), scales=b_scales[:], in_=basis[:]
+                        )
+                        o_cols = slice(g * OUTPUTS, (g + 1) * OUTPUTS)
+                        for m in range(ROW_TILES):
+                            b_cols = slice(m * P, (m + 1) * P)
+                            nc.tensor.matmul_mx(
+                                out=acc[m][:],
+                                lhsT=b_codes[:, b_cols].bitcast(FP8X4),
+                                lhsT_scale=b_scales[:, b_cols],
+                                rhs=w_codes[:, k, o_cols].bitcast(FP8X4),
+                                rhs_scale=w_scales[:, k, o_cols],
+                                start=(g == 0 and k == 0),
+                                stop=(g == HALVES - 1 and k == BASES - 1),
+                            )
+
+            result = stage.tile([P, ROW_TILES, OUTPUTS], F32)
+            for m in range(ROW_TILES):
+                nc.scalar.copy(out=result[:, m, :], in_=acc[m][:])
+            nc.sync.dma_start(
+                out=out[r * ROWS : (r + 1) * ROWS, :].rearrange("(m p) o -> p m o", p=P),
+                in_=result[:],
+            )

@@ -92,22 +92,7 @@ def tile_kanlayer_kernel(tc, x, knots, control_points, out):
         make_identity(nc, ident[:])
         c = spline_constants(nc, consts, knots)
 
-        def load_rows(r):
-            tiles = []
-            for m in range(ROW_TILES):
-                x_sb = x_pool.tile([P, FEATURES], BF16, name="x_sb")
-                first = r * ROWS + m * P
-                nc.sync.dma_start(out=x_sb[:], in_=x[first : first + P, :])
-                tiles.append(x_sb)
-            return tiles
-
-        x_first = load_rows(0)
-
-        cp_sb = weights.tile([P, FEATURES, POINTS], BF16)
-        nc.sync.dma_start(out=cp_sb[:], in_=control_points)
-        w_codes = weights.tile([P, BASES, HALVES * OUTPUTS], U32, align_bytes=64)
-        w_scales = weights.tile([P, BASES, HALVES * OUTPUTS], U8, align_bytes=64)
-        for k in range(BASES):
+        def quantise_control_points(k):
             w_flip = flip_psum.tile([P, HALVES * PACK, P], BF16, name="flip")
             for n in range(HALVES * PACK):
                 nc.tensor.transpose(w_flip[:, n, :], cp_sb[:, n * P : (n + 1) * P, k], ident[:])
@@ -121,106 +106,141 @@ def tile_kanlayer_kernel(tc, x, knots, control_points, out):
                 in_=w_grouped[:].rearrange("p g o t -> p (g o t)"),
             )
 
-        for r in range(ROUNDS):
-            x_tiles = x_first if r == 0 else load_rows(r)
-            v = stage.tile([P, HALVES, ROWS, PACK], BF16)
+        def load_rows(r):
+            tiles = []
             for m in range(ROW_TILES):
+                x_sb = x_pool.tile([P, FEATURES], BF16, name="x_sb")
+                first = r * ROWS + m * P
+                nc.sync.dma_start(out=x_sb[:], in_=x[first : first + P, :])
+                tiles.append(x_sb)
+            return tiles
+
+        def transposed_rows(x_tiles):
+            v = stage.tile([P, HALVES, ROWS, PACK], BF16, name="v")
+            for m in range(ROW_TILES):
+                x_sb = x_tiles[m]
                 x_flip = flip_psum.tile([P, HALVES * PACK, P], BF16, name="flip")
                 for n in range(HALVES * PACK):
-                    nc.tensor.transpose(
-                        x_flip[:, n, :], x_tiles[m][:, n * P : (n + 1) * P], ident[:]
-                    )
+                    nc.tensor.transpose(x_flip[:, n, :], x_sb[:, n * P : (n + 1) * P], ident[:])
                 nc.scalar.copy(
                     out=v[:, :, m * P : (m + 1) * P, :],
                     in_=x_flip[:].rearrange("p (g t) b -> p g b t", g=HALVES),
                 )
+            return v
 
-            acc = [
-                acc_psum.tile([P, OUTPUTS], F32, name="acc%d" % m) for m in range(ROW_TILES)
-            ]
-            for g in range(HALVES):
-                vg = v[:, g, :, :].rearrange("p b t -> p (b t)")
-                p_cube = {}
-                q_cube = {}
-                left = {}
-                for i in range(KNOTS):
-                    square = cube_pool.tile([P, CHUNK], F32)
-                    nc.scalar.activation(
-                        out=square[:], in_=vg, func=ACT.Square, bias=c["neg_t"][:, i : i + 1]
-                    )
-                    cube = cube_pool.tile([P, CHUNK], F32)
-                    nc.vector.scalar_tensor_tensor(
-                        out=cube[:],
-                        in0=vg,
-                        scalar=c["t"][:, i : i + 1],
-                        in1=square[:],
-                        op0=ALU.subtract,
-                        op1=ALU.mult,
-                    )
-                    if i <= KNOTS - 4:
-                        p_cube[i] = cube_pool.tile([P, CHUNK], F32, name="p_cube")
-                        nc.scalar.activation(
-                            out=p_cube[i][:],
-                            in_=cube[:],
-                            func=ACT.Relu,
-                            scale=c["p_scale"][:, i : i + 1],
-                        )
-                    if i >= 3:
-                        q_cube[i] = cube_pool.tile([P, CHUNK], F32, name="q_cube")
-                        nc.scalar.activation(
-                            out=q_cube[i][:],
-                            in_=cube[:],
-                            func=ACT.Relu,
-                            scale=c["q_scale"][:, i - 3 : i - 2],
-                        )
-                    if 1 <= i <= BASES:
-                        k = i - 1
-                        left[k] = left_pool.tile([P, CHUNK], BF16, name="left")
-                        nc.vector.scalar_tensor_tensor(
-                            out=left[k][:],
-                            in0=p_cube[k + 1][:],
-                            scalar=c["left_w"][:, k : k + 1],
-                            in1=p_cube[k][:],
-                            op0=ALU.mult,
-                            op1=ALU.add,
-                        )
-                    if i >= 4:
-                        k = i - 4
-                        right = stage.tile([P, CHUNK], BF16)
-                        nc.vector.scalar_tensor_tensor(
-                            out=right[:],
-                            in0=q_cube[k + 3][:],
-                            scalar=c["right_w"][:, k : k + 1],
-                            in1=q_cube[k + 4][:],
-                            op0=ALU.mult,
-                            op1=ALU.add,
-                        )
-                        basis = mx_pool.tile([P, CHUNK], BF16, align_bytes=64)
-                        nc.vector.tensor_tensor(
-                            out=basis[:], in0=left[k][:], in1=right[:], op=ALU.max
-                        )
-                        b_codes = mx_pool.tile([P, ROWS], U32, align_bytes=64)
-                        b_scales = mx_pool.tile([P, ROWS], U8, align_bytes=64)
-                        nc.vector.quantize_mx(
-                            out=b_codes[:].bitcast(FP8X4), scales=b_scales[:], in_=basis[:]
-                        )
-                        o_cols = slice(g * OUTPUTS, (g + 1) * OUTPUTS)
-                        for m in range(ROW_TILES):
-                            b_cols = slice(m * P, (m + 1) * P)
-                            nc.tensor.matmul_mx(
-                                out=acc[m][:],
-                                lhsT=b_codes[:, b_cols].bitcast(FP8X4),
-                                lhsT_scale=b_scales[:, b_cols],
-                                rhs=w_codes[:, k, o_cols].bitcast(FP8X4),
-                                rhs_scale=w_scales[:, k, o_cols],
-                                start=(g == 0 and k == 0),
-                                stop=(g == HALVES - 1 and k == BASES - 1),
-                            )
+        def signed_cube(vg, i):
+            square = cube_pool.tile([P, CHUNK], F32, name="square")
+            nc.scalar.activation(
+                out=square[:], in_=vg, func=ACT.Square, bias=c["neg_t"][:, i : i + 1]
+            )
+            cube = cube_pool.tile([P, CHUNK], F32, name="cube")
+            nc.vector.scalar_tensor_tensor(
+                out=cube[:],
+                in0=vg,
+                scalar=c["t"][:, i : i + 1],
+                in1=square[:],
+                op0=ALU.subtract,
+                op1=ALU.mult,
+            )
+            return cube
 
-            result = stage.tile([P, ROW_TILES, OUTPUTS], F32)
+        def use_cube(cube, i, g, side, acc):
+            p_cube, q_cube, left = side
+            if i <= KNOTS - 4:
+                p_cube[i] = cube_pool.tile([P, CHUNK], F32, name="p_cube")
+                nc.scalar.activation(
+                    out=p_cube[i][:], in_=cube[:], func=ACT.Relu, scale=c["p_scale"][:, i : i + 1]
+                )
+            if i >= 3:
+                q_cube[i] = cube_pool.tile([P, CHUNK], F32, name="q_cube")
+                nc.scalar.activation(
+                    out=q_cube[i][:],
+                    in_=cube[:],
+                    func=ACT.Relu,
+                    scale=c["q_scale"][:, i - 3 : i - 2],
+                )
+            if 1 <= i <= BASES:
+                k = i - 1
+                left[k] = left_pool.tile([P, CHUNK], BF16, name="left")
+                nc.vector.scalar_tensor_tensor(
+                    out=left[k][:],
+                    in0=p_cube[k + 1][:],
+                    scalar=c["left_w"][:, k : k + 1],
+                    in1=p_cube[k][:],
+                    op0=ALU.mult,
+                    op1=ALU.add,
+                )
+            if i >= 4:
+                k = i - 4
+                right = stage.tile([P, CHUNK], BF16, name="right")
+                nc.vector.scalar_tensor_tensor(
+                    out=right[:],
+                    in0=q_cube[k + 3][:],
+                    scalar=c["right_w"][:, k : k + 1],
+                    in1=q_cube[k + 4][:],
+                    op0=ALU.mult,
+                    op1=ALU.add,
+                )
+                basis = mx_pool.tile([P, CHUNK], BF16, align_bytes=64, name="basis")
+                nc.vector.tensor_tensor(out=basis[:], in0=left[k][:], in1=right[:], op=ALU.max)
+                b_codes = mx_pool.tile([P, ROWS], U32, align_bytes=64, name="b_codes")
+                b_scales = mx_pool.tile([P, ROWS], U8, align_bytes=64, name="b_scales")
+                nc.vector.quantize_mx(
+                    out=b_codes[:].bitcast(FP8X4), scales=b_scales[:], in_=basis[:]
+                )
+                o_cols = slice(g * OUTPUTS, (g + 1) * OUTPUTS)
+                for m in range(ROW_TILES):
+                    b_cols = slice(m * P, (m + 1) * P)
+                    nc.tensor.matmul_mx(
+                        out=acc[m][:],
+                        lhsT=b_codes[:, b_cols].bitcast(FP8X4),
+                        lhsT_scale=b_scales[:, b_cols],
+                        rhs=w_codes[:, k, o_cols].bitcast(FP8X4),
+                        rhs_scale=w_scales[:, k, o_cols],
+                        start=(g == 0 and k == 0),
+                        stop=(g == HALVES - 1 and k == BASES - 1),
+                    )
+
+        def store_round(r, acc):
+            result = stage.tile([P, ROW_TILES, OUTPUTS], F32, name="result")
             for m in range(ROW_TILES):
                 nc.scalar.copy(out=result[:, m, :], in_=acc[m][:])
             nc.sync.dma_start(
                 out=out[r * ROWS : (r + 1) * ROWS, :].rearrange("(m p) o -> p m o", p=P),
                 in_=result[:],
             )
+
+        w_codes = weights.tile([P, BASES, HALVES * OUTPUTS], U32, align_bytes=64)
+        w_scales = weights.tile([P, BASES, HALVES * OUTPUTS], U8, align_bytes=64)
+
+        ctx.enter_context(tc.manual_schedule())
+        x_tiles = {0: load_rows(0)}
+        cp_sb = weights.tile([P, FEATURES, POINTS], BF16)
+        nc.sync.dma_start(out=cp_sb[:], in_=control_points)
+        v_tiles = {0: transposed_rows(x_tiles[0])}
+        waiting = None
+        acc = None
+        for r in range(ROUNDS):
+            for g in range(HALVES):
+                vg = v_tiles[r][:, g, :, :].rearrange("p b t -> p (b t)")
+                side = ({}, {}, {})
+                for i in range(KNOTS):
+                    cube = signed_cube(vg, i)
+                    if r == 0 and g == 0 and 3 <= i < 3 + BASES:
+                        quantise_control_points(i - 3)
+                    if waiting is not None:
+                        use_cube(*waiting)
+                        if waiting[1] == KNOTS - 1 and waiting[2] == HALVES - 1:
+                            store_round(r - 1, waiting[4])
+                    if g == 0 and i == 0:
+                        acc = [
+                            acc_psum.tile([P, OUTPUTS], F32, name="acc%d" % m)
+                            for m in range(ROW_TILES)
+                        ]
+                    waiting = (cube, i, g, side, acc)
+                    if g == 0 and i == 0 and r + 1 < ROUNDS:
+                        x_tiles[r + 1] = load_rows(r + 1)
+                    if g == HALVES - 1 and i == 0 and r + 1 < ROUNDS:
+                        v_tiles[r + 1] = transposed_rows(x_tiles[r + 1])
+        use_cube(*waiting)
+        store_round(ROUNDS - 1, waiting[4])

from contextlib import ExitStack

import concourse.mybir as mybir
from concourse.masks import make_identity

F32 = mybir.dt.float32
BF16 = mybir.dt.bfloat16
U32 = mybir.dt.uint32
U8 = mybir.dt.uint8
FP8X4 = mybir.dt.float8_e4m3fn_x4
ALU = mybir.AluOpType
ACT = mybir.ActivationFunctionType

P = 128
PACK = 4
BATCH = 2048
FEATURES = 1024
OUTPUTS = 128
KNOTS = 14
POINTS = 13
BASES = 10
HALVES = FEATURES // (P * PACK)
ROWS = 512
ROW_TILES = ROWS // P
ROUNDS = BATCH // ROWS
CHUNK = ROWS * PACK

FLOPS = 2 * BATCH * BASES * FEATURES * OUTPUTS


def spline_constants(nc, pool, knots):
    knots_bf = pool.tile([P, KNOTS], BF16)
    nc.sync.dma_start(out=knots_bf[:], in_=knots.partition_broadcast(P))
    t = pool.tile([P, KNOTS], F32)
    nc.vector.tensor_copy(out=t[:], in_=knots_bf[:])
    neg_t = pool.tile([P, KNOTS], F32)
    nc.vector.tensor_scalar_mul(out=neg_t[:], in0=t[:], scalar1=-1.0)

    d1 = pool.tile([P, KNOTS - 1], F32)
    d2 = pool.tile([P, KNOTS - 2], F32)
    d3 = pool.tile([P, KNOTS - 3], F32)
    d4 = pool.tile([P, KNOTS - 4], F32)
    for step, diff in ((1, d1), (2, d2), (3, d3), (4, d4)):
        nc.vector.tensor_sub(out=diff[:], in0=t[:, step:KNOTS], in1=t[:, 0 : KNOTS - step])

    cubes = KNOTS - 3
    p_prod = pool.tile([P, cubes], F32)
    nc.vector.tensor_mul(out=p_prod[:], in0=d1[:, 0:cubes], in1=d2[:, 0:cubes])
    nc.vector.tensor_mul(out=p_prod[:], in0=p_prod[:], in1=d3[:, 0:cubes])
    p_scale = pool.tile([P, cubes], F32)
    nc.vector.reciprocal(out=p_scale[:], in_=p_prod[:])
    q_prod = pool.tile([P, cubes], F32)
    nc.vector.tensor_mul(out=q_prod[:], in0=d1[:, 2 : 2 + cubes], in1=d2[:, 1 : 1 + cubes])
    nc.vector.tensor_mul(out=q_prod[:], in0=q_prod[:], in1=d3[:, 0:cubes])
    q_recip = pool.tile([P, cubes], F32)
    nc.vector.reciprocal(out=q_recip[:], in_=q_prod[:])
    q_scale = pool.tile([P, cubes], F32)
    nc.vector.tensor_scalar_mul(out=q_scale[:], in0=q_recip[:], scalar1=-1.0)

    d1_recip = pool.tile([P, KNOTS - 1], F32)
    nc.vector.reciprocal(out=d1_recip[:], in_=d1[:])
    neg_d4 = pool.tile([P, BASES], F32)
    nc.vector.tensor_scalar_mul(out=neg_d4[:], in0=d4[:], scalar1=-1.0)
    left_w = pool.tile([P, BASES], F32)
    nc.vector.tensor_mul(out=left_w[:], in0=neg_d4[:], in1=d1_recip[:, 0:BASES])
    right_w = pool.tile([P, BASES], F32)
    nc.vector.tensor_mul(out=right_w[:], in0=neg_d4[:], in1=d1_recip[:, 3 : 3 + BASES])
    return {
        "t": t,
        "neg_t": neg_t,
        "p_scale": p_scale,
        "q_scale": q_scale,
        "left_w": left_w,
        "right_w": right_w,
    }


def tile_kanlayer_kernel(tc, x, knots, control_points, out):
    nc = tc.nc
    with ExitStack() as ctx:
        consts = ctx.enter_context(tc.tile_pool(name="consts", bufs=1))
        weights = ctx.enter_context(tc.tile_pool(name="weights", bufs=1))
        stage = ctx.enter_context(tc.tile_pool(name="stage", bufs=2))
        x_pool = ctx.enter_context(tc.tile_pool(name="x_pool", bufs=ROW_TILES))
        cube_pool = ctx.enter_context(tc.tile_pool(name="cube_pool", bufs=3))
        left_pool = ctx.enter_context(tc.tile_pool(name="left_pool", bufs=6))
        mx_pool = ctx.enter_context(tc.tile_pool(name="mx_pool", bufs=3))
        flip_psum = ctx.enter_context(tc.psum_pool(name="flip_psum", bufs=3))
        acc_psum = ctx.enter_context(tc.psum_pool(name="acc_psum", bufs=1))

        ident = consts.tile([P, P], BF16)
        make_identity(nc, ident[:])
        c = spline_constants(nc, consts, knots)

        def quantise_control_points(k):
            w_flip = flip_psum.tile([P, HALVES * PACK, P], BF16, name="flip")
            for n in range(HALVES * PACK):
                nc.tensor.transpose(w_flip[:, n, :], cp_sb[:, n * P : (n + 1) * P, k], ident[:])
            w_grouped = stage.tile([P, HALVES, OUTPUTS, PACK], BF16, align_bytes=64)
            nc.scalar.copy(
                out=w_grouped[:], in_=w_flip[:].rearrange("p (g t) o -> p g o t", g=HALVES)
            )
            nc.vector.quantize_mx(
                out=w_codes[:, k, :].bitcast(FP8X4),
                scales=w_scales[:, k, :],
                in_=w_grouped[:].rearrange("p g o t -> p (g o t)"),
            )

        def load_rows(r):
            tiles = []
            for m in range(ROW_TILES):
                x_sb = x_pool.tile([P, FEATURES], BF16, name="x_sb")
                first = r * ROWS + m * P
                nc.sync.dma_start(out=x_sb[:], in_=x[first : first + P, :])
                tiles.append(x_sb)
            return tiles

        def transposed_rows(x_tiles):
            v = stage.tile([P, HALVES, ROWS, PACK], BF16, name="v")
            for m in range(ROW_TILES):
                x_sb = x_tiles[m]
                x_flip = flip_psum.tile([P, HALVES * PACK, P], BF16, name="flip")
                for n in range(HALVES * PACK):
                    nc.tensor.transpose(x_flip[:, n, :], x_sb[:, n * P : (n + 1) * P], ident[:])
                nc.scalar.copy(
                    out=v[:, :, m * P : (m + 1) * P, :],
                    in_=x_flip[:].rearrange("p (g t) b -> p g b t", g=HALVES),
                )
            return v

        def signed_cube(vg, i):
            square = cube_pool.tile([P, CHUNK], F32, name="square")
            nc.scalar.activation(
                out=square[:], in_=vg, func=ACT.Square, bias=c["neg_t"][:, i : i + 1]
            )
            cube = cube_pool.tile([P, CHUNK], F32, name="cube")
            nc.vector.scalar_tensor_tensor(
                out=cube[:],
                in0=vg,
                scalar=c["t"][:, i : i + 1],
                in1=square[:],
                op0=ALU.subtract,
                op1=ALU.mult,
            )
            return cube

        def use_cube(cube, i, g, side, acc):
            p_cube, q_cube, left = side
            if i <= KNOTS - 4:
                p_cube[i] = cube_pool.tile([P, CHUNK], F32, name="p_cube")
                nc.scalar.activation(
                    out=p_cube[i][:], in_=cube[:], func=ACT.Relu, scale=c["p_scale"][:, i : i + 1]
                )
            if i >= 3:
                q_cube[i] = cube_pool.tile([P, CHUNK], F32, name="q_cube")
                nc.scalar.activation(
                    out=q_cube[i][:],
                    in_=cube[:],
                    func=ACT.Relu,
                    scale=c["q_scale"][:, i - 3 : i - 2],
                )
            if 1 <= i <= BASES:
                k = i - 1
                left[k] = left_pool.tile([P, CHUNK], BF16, name="left")
                nc.vector.scalar_tensor_tensor(
                    out=left[k][:],
                    in0=p_cube[k + 1][:],
                    scalar=c["left_w"][:, k : k + 1],
                    in1=p_cube[k][:],
                    op0=ALU.mult,
                    op1=ALU.add,
                )
            if i >= 4:
                k = i - 4
                right = stage.tile([P, CHUNK], BF16, name="right")
                nc.vector.scalar_tensor_tensor(
                    out=right[:],
                    in0=q_cube[k + 3][:],
                    scalar=c["right_w"][:, k : k + 1],
                    in1=q_cube[k + 4][:],
                    op0=ALU.mult,
                    op1=ALU.add,
                )
                basis = mx_pool.tile([P, CHUNK], BF16, align_bytes=64, name="basis")
                nc.vector.tensor_tensor(out=basis[:], in0=left[k][:], in1=right[:], op=ALU.max)
                b_codes = mx_pool.tile([P, ROWS], U32, align_bytes=64, name="b_codes")
                b_scales = mx_pool.tile([P, ROWS], U8, align_bytes=64, name="b_scales")
                nc.vector.quantize_mx(
                    out=b_codes[:].bitcast(FP8X4), scales=b_scales[:], in_=basis[:]
                )
                o_cols = slice(g * OUTPUTS, (g + 1) * OUTPUTS)
                for m in range(ROW_TILES):
                    b_cols = slice(m * P, (m + 1) * P)
                    nc.tensor.matmul_mx(
                        out=acc[m][:],
                        lhsT=b_codes[:, b_cols].bitcast(FP8X4),
                        lhsT_scale=b_scales[:, b_cols],
                        rhs=w_codes[:, k, o_cols].bitcast(FP8X4),
                        rhs_scale=w_scales[:, k, o_cols],
                        start=(g == 0 and k == 0),
                        stop=(g == HALVES - 1 and k == BASES - 1),
                    )

        def store_round(r, acc):
            result = stage.tile([P, ROW_TILES, OUTPUTS], F32, name="result")
            for m in range(ROW_TILES):
                nc.scalar.copy(out=result[:, m, :], in_=acc[m][:])
            nc.sync.dma_start(
                out=out[r * ROWS : (r + 1) * ROWS, :].rearrange("(m p) o -> p m o", p=P),
                in_=result[:],
            )

        w_codes = weights.tile([P, BASES, HALVES * OUTPUTS], U32, align_bytes=64)
        w_scales = weights.tile([P, BASES, HALVES * OUTPUTS], U8, align_bytes=64)

        ctx.enter_context(tc.manual_schedule())
        x_tiles = {0: load_rows(0)}
        cp_sb = weights.tile([P, FEATURES, POINTS], BF16)
        nc.sync.dma_start(out=cp_sb[:], in_=control_points)
        v_tiles = {0: transposed_rows(x_tiles[0])}
        waiting = None
        acc = None
        for r in range(ROUNDS):
            for g in range(HALVES):
                vg = v_tiles[r][:, g, :, :].rearrange("p b t -> p (b t)")
                side = ({}, {}, {})
                for i in range(KNOTS):
                    cube = signed_cube(vg, i)
                    if r == 0 and g == 0 and 3 <= i < 3 + BASES:
                        quantise_control_points(i - 3)
                    if waiting is not None:
                        use_cube(*waiting)
                        if waiting[1] == KNOTS - 1 and waiting[2] == HALVES - 1:
                            store_round(r - 1, waiting[4])
                    if g == 0 and i == 0:
                        acc = [
                            acc_psum.tile([P, OUTPUTS], F32, name="acc%d" % m)
                            for m in range(ROW_TILES)
                        ]
                    waiting = (cube, i, g, side, acc)
                    if g == 0 and i == 0 and r + 1 < ROUNDS:
                        x_tiles[r + 1] = load_rows(r + 1)
                    if g == HALVES - 1 and i == 0 and r + 1 < ROUNDS:
                        v_tiles[r + 1] = transposed_rows(x_tiles[r + 1])
        use_cube(*waiting)
        store_round(ROUNDS - 1, waiting[4])
